import numpy as np
import ml_dtypes


def mxq(x, axis, fmt="e4m3"):
    dtype, down = {"e4m3": (ml_dtypes.float8_e4m3fn, 7), "e5m2": (ml_dtypes.float8_e5m2, 14)}[fmt]
    v = np.moveaxis(np.asarray(x, np.float32).astype(ml_dtypes.bfloat16).astype(np.float64), axis, -1)
    blocks = v.reshape(v.shape[:-1] + (-1, 32))
    amax = np.abs(blocks).max(-1, keepdims=True)
    byte = np.maximum(np.where(amax > 0, np.frexp(amax)[1] - 1 + 127, 0) - down, 1)
    scale = np.exp2(byte - 127.0)
    codes = (blocks / scale).astype(np.float32).astype(dtype).astype(np.float64)
    return np.moveaxis((codes * scale).reshape(v.shape), -1, axis)


WIDE = False


def mx_kscale(k):
    if not WIDE:
        return np.ones(k)
    levels = np.array([10, -10, 5, -5, 0])
    a = np.random.permutation(np.resize(levels, k // 512 * 4)).reshape(k // 512, 4)
    idx = np.arange(k)
    return np.exp2(a[idx // 512, idx % 128 // 32])


BF16 = ml_dtypes.bfloat16


def bf(x):
    return np.asarray(x, np.float32).astype(BF16)


def f64(x):
    return np.asarray(x).astype(np.float64)


E2M1 = np.array([0.0, 0.5, 1.0, 1.5, 2.0, 3.0, 4.0, 6.0, -0.0, -0.5, -1.0, -1.5, -2.0, -3.0, -4.0, -6.0])


def pack_weight(w, fmt):
    k, n = w.shape
    w = f64(bf(w)).reshape(k // 32, 32, n)
    amax = np.abs(w).max(1)
    if fmt == "e4m3":
        byte = np.frexp(amax)[1] - 1 + 127 - 7
    else:
        mant, ex = np.frexp(amax / 6.0)
        byte = np.where(mant > 0.5, ex, ex - 1) + 127
    byte = np.clip(np.where(amax > 0, byte, 1), 1, 254)
    scaled = (w * np.exp2(127.0 - byte)[:, None, :]).reshape(k, n).astype(np.float32)
    by_word = np.ascontiguousarray(scaled.reshape(k // 512, 128, 4, n).transpose(0, 1, 3, 2))
    if fmt == "e4m3":
        words = by_word.astype(ml_dtypes.float8_e4m3fn).view(np.uint8)
    else:
        c = by_word.astype(ml_dtypes.float4_e2m1fn).view(np.uint8) & 0xF
        words = c[..., 0::2] | (c[..., 1::2] << 4)
    return np.ascontiguousarray(words), np.ascontiguousarray(byte.astype(np.uint8).reshape(k // 512, 16, n))


def unpack_weight(words, scales, fmt):
    g, p, n, _ = words.shape
    if fmt == "e4m3":
        vals = np.ascontiguousarray(words).view(ml_dtypes.float8_e4m3fn).astype(np.float64)
    else:
        nib = np.empty((g, p, n, 4), np.uint8)
        nib[..., 0::2] = words & 0xF
        nib[..., 1::2] = words >> 4
        vals = E2M1[nib]
    vals = vals * np.repeat(np.exp2(scales.astype(np.float64) - 127.0), 8, axis=1)[..., None]
    return vals.transpose(0, 1, 3, 2).reshape(g * 512, n)


B, K, N = 128, 2048, 2048


def setup_inputs():
    s = mx_kscale(K)
    x = bf(np.random.standard_normal((B, K)) * s)
    dft_real = np.random.standard_normal((N, K)) / np.sqrt(K) / s[None, :]
    dft_imag = np.random.standard_normal((N, K)) / np.sqrt(K) / s[None, :]
    dft_real_words, dft_real_scales = pack_weight(dft_real.T, "e4m3")
    dft_imag_words, dft_imag_scales = pack_weight(dft_imag.T, "e4m3")
    return {"x": x,
            "dft_real_words": dft_real_words,
            "dft_real_scales": dft_real_scales,
            "dft_imag_words": dft_imag_words,
            "dft_imag_scales": dft_imag_scales}


def reference(x, dft_real_words, dft_real_scales, dft_imag_words, dft_imag_scales):
    xq = mxq(f64(x), 1, "e4m3")
    rxs = xq @ unpack_weight(dft_real_words, dft_real_scales, "e4m3")
    ixs = xq @ unpack_weight(dft_imag_words, dft_imag_scales, "e4m3")
    mag = np.log(rxs * rxs + ixs * ixs)
    return mag

@@ -1,0 +1,129 @@
+from contextlib import ExitStack
+
+import concourse.mybir as mybir
+from concourse.masks import make_identity
+
+F32 = mybir.dt.float32
+BF16 = mybir.dt.bfloat16
+I32 = mybir.dt.int32
+U32 = mybir.dt.uint32
+U8 = mybir.dt.uint8
+FP8X4 = mybir.dt.float8_e4m3fn_x4
+ACT = mybir.ActivationFunctionType
+ALU = mybir.AluOpType
+
+P = 128
+K = 2048
+N = 2048
+GROUPS = K // 512
+N_TILE = 512
+N_TILES = N // N_TILE
+FLOPS = 2 * 2 * P * K * N
+
+
+def tile_dft_w_kernel(tc, x, real_words, real_scales, imag_words, imag_scales, out):
+    nc = tc.nc
+    words = (real_words, imag_words)
+    scales = (real_scales, imag_scales)
+    with ExitStack() as ctx:
+        keep = ctx.enter_context(tc.tile_pool(name="keep", bufs=1))
+        work = ctx.enter_context(tc.tile_pool(name="work", bufs=3))
+        psum_t = ctx.enter_context(tc.psum_pool(name="psum_t", bufs=2))
+        psum_a = ctx.enter_context(tc.psum_pool(name="psum_a", bufs=3))
+
+        x_sb = keep.tile([P, K], BF16, align_bytes=64)
+        nc.sync.dma_start(out=x_sb[:], in_=x)
+
+        planes = keep.tile([P, 2, N], U8, align_bytes=64)
+        nc.vector.memset(planes[:].rearrange("p w n -> p (w n)").bitcast(I32), 0)
+
+        one = keep.tile([P, 1], F32)
+        nc.vector.memset(one[:], 1.0)
+        warm = keep.tile([P, 1], F32)
+        nc.scalar.activation(out=warm[:], in_=one[:], func=ACT.Ln)
+
+        ident = keep.tile([P, P], F32)
+        make_identity(nc, ident[:])
+
+        for w in range(2):
+            for q in range(4):
+                nc.sync.dma_start(
+                    out=planes[32 * q : 32 * q + 16, w, :].bitcast(I32),
+                    in_=scales[w][:, 4 * q : 4 * q + 4, :].bitcast(I32),
+                )
+
+        pieces = {}
+        for j in range(N_TILES):
+            for w in range(2):
+                view = words[w].rearrange("g p n t -> p g (n t)")
+                cuts = [(0, GROUPS)]
+                if j == N_TILES - 1 and w == 1:
+                    cuts = [(0, GROUPS - 1), (GROUPS - 1, 1)]
+                pieces[(w, j)] = []
+                for g0, ng in cuts:
+                    wt = keep.tile([P, ng, N_TILE], U32, name="w%d_%d_%d" % (w, j, g0), align_bytes=64)
+                    nc.sync.dma_start(
+                        out=wt[:].bitcast(I32),
+                        in_=view[:, g0 : g0 + ng, 4 * N_TILE * j : 4 * N_TILE * (j + 1)].bitcast(I32),
+                    )
+                    pieces[(w, j)].append((wt, g0, ng))
+
+        xw = x_sb[:].bitcast(F32)
+        grouped = keep.tile([P, K], BF16, align_bytes=64)
+        grouped_w = grouped[:].bitcast(F32)
+        x_codes = keep.tile([P, GROUPS * P], U32, align_bytes=64)
+        x_plane = keep.tile([P, GROUPS * P], U8, align_bytes=64)
+        for h in range(2):
+            xt = psum_t.tile([P, 4, P], F32, tag="xt")
+            for gl in range(2):
+                g = 2 * h + gl
+                for u in range(2):
+                    nc.tensor.transpose(xt[:, 2 * gl + u, :], xw[:, 256 * g + u : 256 * (g + 1) : 2], ident[:])
+            dst = grouped_w[:, 512 * h : 512 * (h + 1)].rearrange("p (g b u) -> p g b u", g=2, u=2)
+            src = xt[:].rearrange("p (g u) b -> p g b u", u=2)
+            if h == 0:
+                nc.vector.tensor_copy(out=dst, in_=src)
+            else:
+                nc.scalar.copy(out=dst, in_=src)
+        for h in range(2):
+            nc.vector.quantize_mx(
+                out=x_codes[:, 256 * h : 256 * (h + 1)].bitcast(FP8X4),
+                scales=x_plane[:, 256 * h : 256 * (h + 1)],
+                in_=grouped[:, 1024 * h : 1024 * (h + 1)],
+            )
+
+        def project(w, j, acc):
+            for wt, g0, ng in pieces[(w, j)]:
+                for gl in range(ng):
+                    g = g0 + gl
+                    nc.tensor.matmul_mx(
+                        out=acc[:],
+                        lhsT=x_codes[:, P * g : P * (g + 1)].bitcast(FP8X4),
+                        lhsT_scale=x_plane[:, P * g : P * (g + 1)],
+                        rhs=wt[:, gl, :].bitcast(FP8X4),
+                        rhs_scale=planes[4 * g : P, w, N_TILE * j : N_TILE * (j + 1)],
+                        start=(g == 0),
+                        stop=(g == GROUPS - 1),
+                    )
+
+        for j in range(N_TILES):
+            parts = 2 if j == N_TILES - 1 else 1
+            width = N_TILE // parts
+            pr = psum_a.tile([P, N_TILE], F32, tag="pr")
+            project(0, j, pr)
+            sq_r = work.tile([P, N_TILE], F32, tag="sq_r")
+            nc.scalar.activation(out=sq_r[:], in_=pr[:], func=ACT.Square)
+            pi = psum_a.tile([P, N_TILE], F32, tag="pi")
+            project(1, j, pi)
+            sq_i = work.tile([P, N_TILE], F32, tag="sq_i")
+            res = work.tile([P, N_TILE], F32, tag="res")
+            for c in range(parts):
+                cols = slice(width * c, width * (c + 1))
+                nc.scalar.activation(out=sq_i[:, cols], in_=pi[:, cols], func=ACT.Square)
+            for c in range(parts):
+                cols = slice(width * c, width * (c + 1))
+                nc.vector.tensor_tensor(out=sq_i[:, cols], in0=sq_i[:, cols], in1=sq_r[:, cols], op=ALU.add)
+                nc.scalar.activation(out=res[:, cols], in_=sq_i[:, cols], func=ACT.Ln)
+                nc.scalar.dma_start(
+                    out=out[:, N_TILE * j + width * c : N_TILE * j + width * (c + 1)], in_=res[:, cols]
+                )

@@ -18,6 +18,7 @@ N = 2048
 GROUPS = K // 512
 N_TILE = 512
 N_TILES = N // N_TILE
+WHOLE = 5
 FLOPS = 2 * 2 * P * K * N
 
 
@@ -28,8 +29,7 @@ def tile_dft_w_kernel(tc, x, real_words, real_scales, imag_words, imag_scales, o
     with ExitStack() as ctx:
         keep = ctx.enter_context(tc.tile_pool(name="keep", bufs=1))
         work = ctx.enter_context(tc.tile_pool(name="work", bufs=3))
-        psum_t = ctx.enter_context(tc.psum_pool(name="psum_t", bufs=2))
-        psum_a = ctx.enter_context(tc.psum_pool(name="psum_a", bufs=3))
+        psum = ctx.enter_context(tc.psum_pool(name="psum", bufs=1))
 
         x_sb = keep.tile([P, K], BF16, align_bytes=64)
         nc.sync.dma_start(out=x_sb[:], in_=x)
@@ -52,21 +52,21 @@ def tile_dft_w_kernel(tc, x, real_words, real_scales, imag_words, imag_scales, o
                     in_=scales[w][:, 4 * q : 4 * q + 4, :].bitcast(I32),
                 )
 
-        pieces = {}
+        rhs = {}
+        order = [(w, g) for g in range(GROUPS) for w in range(2)]
+        for w, g in order[:WHOLE]:
+            wt = keep.tile([P, N], U32, name="whole%d_%d" % (w, g), align_bytes=64)
+            nc.sync.dma_start(out=wt[:].bitcast(I32), in_=words[w][g].rearrange("p n t -> p (n t)").bitcast(I32))
+            for j in range(N_TILES):
+                rhs[(w, g, j)] = wt[:, N_TILE * j : N_TILE * (j + 1)]
         for j in range(N_TILES):
-            for w in range(2):
-                view = words[w].rearrange("g p n t -> p g (n t)")
-                cuts = [(0, GROUPS)]
-                if j == N_TILES - 1 and w == 1:
-                    cuts = [(0, GROUPS - 1), (GROUPS - 1, 1)]
-                pieces[(w, j)] = []
-                for g0, ng in cuts:
-                    wt = keep.tile([P, ng, N_TILE], U32, name="w%d_%d_%d" % (w, j, g0), align_bytes=64)
-                    nc.sync.dma_start(
-                        out=wt[:].bitcast(I32),
-                        in_=view[:, g0 : g0 + ng, 4 * N_TILE * j : 4 * N_TILE * (j + 1)].bitcast(I32),
-                    )
-                    pieces[(w, j)].append((wt, g0, ng))
+            for w, g in order[WHOLE:]:
+                wt = keep.tile([P, N_TILE], U32, name="late%d_%d_%d" % (w, g, j), align_bytes=64)
+                nc.sync.dma_start(
+                    out=wt[:].bitcast(I32),
+                    in_=words[w][g].rearrange("p n t -> p (n t)")[:, 4 * N_TILE * j : 4 * N_TILE * (j + 1)].bitcast(I32),
+                )
+                rhs[(w, g, j)] = wt[:]
 
         xw = x_sb[:].bitcast(F32)
         grouped = keep.tile([P, K], BF16, align_bytes=64)
@@ -74,7 +74,7 @@ def tile_dft_w_kernel(tc, x, real_words, real_scales, imag_words, imag_scales, o
         x_codes = keep.tile([P, GROUPS * P], U32, align_bytes=64)
         x_plane = keep.tile([P, GROUPS * P], U8, align_bytes=64)
         for h in range(2):
-            xt = psum_t.tile([P, 4, P], F32, tag="xt")
+            xt = psum.tile([P, 4, P], F32, tag="acc1_%d" % (2 + h), name="xt%d" % h)
             for gl in range(2):
                 g = 2 * h + gl
                 for u in range(2):
@@ -92,38 +92,41 @@ def tile_dft_w_kernel(tc, x, real_words, real_scales, imag_words, imag_scales, o
                 in_=grouped[:, 1024 * h : 1024 * (h + 1)],
             )
 
-        def project(w, j, acc):
-            for wt, g0, ng in pieces[(w, j)]:
-                for gl in range(ng):
-                    g = g0 + gl
-                    nc.tensor.matmul_mx(
-                        out=acc[:],
-                        lhsT=x_codes[:, P * g : P * (g + 1)].bitcast(FP8X4),
-                        lhsT_scale=x_plane[:, P * g : P * (g + 1)],
-                        rhs=wt[:, gl, :].bitcast(FP8X4),
-                        rhs_scale=planes[4 * g : P, w, N_TILE * j : N_TILE * (j + 1)],
-                        start=(g == 0),
-                        stop=(g == GROUPS - 1),
-                    )
+        acc = {}
+        for w in range(2):
+            for j in range(N_TILES):
+                acc[(w, j)] = psum.tile([P, N_TILE], F32, tag="acc%d_%d" % (w, j), name="acc%d_%d" % (w, j))
+
+        def mx_pass(w, g, j):
+            nc.tensor.matmul_mx(
+                out=acc[(w, j)][:],
+                lhsT=x_codes[:, P * g : P * (g + 1)].bitcast(FP8X4),
+                lhsT_scale=x_plane[:, P * g : P * (g + 1)],
+                rhs=rhs[(w, g, j)].bitcast(FP8X4),
+                rhs_scale=planes[4 * g : P, w, N_TILE * j : N_TILE * (j + 1)],
+                start=(g == 0),
+                stop=(g == GROUPS - 1),
+            )
+
+        for w, g in order[:WHOLE]:
+            for j in range(N_TILES):
+                mx_pass(w, g, j)
 
         for j in range(N_TILES):
             parts = 2 if j == N_TILES - 1 else 1
             width = N_TILE // parts
-            pr = psum_a.tile([P, N_TILE], F32, tag="pr")
-            project(0, j, pr)
-            sq_r = work.tile([P, N_TILE], F32, tag="sq_r")
-            nc.scalar.activation(out=sq_r[:], in_=pr[:], func=ACT.Square)
-            pi = psum_a.tile([P, N_TILE], F32, tag="pi")
-            project(1, j, pi)
-            sq_i = work.tile([P, N_TILE], F32, tag="sq_i")
+            sq = [work.tile([P, N_TILE], F32, tag="sq%d" % w, name="sq%d_%d" % (w, j)) for w in range(2)]
             res = work.tile([P, N_TILE], F32, tag="res")
+            for w, g in order[WHOLE:]:
+                mx_pass(w, g, j)
+                if g == GROUPS - 1:
+                    for c in range(parts):
+                        cols = slice(width * c, width * (c + 1))
+                        nc.scalar.activation(out=sq[w][:, cols], in_=acc[(w, j)][:, cols], func=ACT.Square)
             for c in range(parts):
                 cols = slice(width * c, width * (c + 1))
-                nc.scalar.activation(out=sq_i[:, cols], in_=pi[:, cols], func=ACT.Square)
-            for c in range(parts):
-                cols = slice(width * c, width * (c + 1))
-                nc.vector.tensor_tensor(out=sq_i[:, cols], in0=sq_i[:, cols], in1=sq_r[:, cols], op=ALU.add)
-                nc.scalar.activation(out=res[:, cols], in_=sq_i[:, cols], func=ACT.Ln)
+                nc.vector.tensor_tensor(out=sq[1][:, cols], in0=sq[1][:, cols], in1=sq[0][:, cols], op=ALU.add)
+                nc.scalar.activation(out=res[:, cols], in_=sq[1][:, cols], func=ACT.Ln)
                 nc.scalar.dma_start(
                     out=out[:, N_TILE * j + width * c : N_TILE * j + width * (c + 1)], in_=res[:, cols]
                 )

@@ -16,9 +16,10 @@ P = 128
 K = 2048
 N = 2048
 GROUPS = K // 512
-N_TILE = 512
-N_TILES = N // N_TILE
-WHOLE = 5
+BANK = 512
+REAL, IMAG = 0, 1
+WHOLE_IMAG = 1
+IMAG_RANGES = [(0, 512), (512, 512), (1024, 512), (1536, 256), (1792, 256)]
 FLOPS = 2 * 2 * P * K * N
 
 
@@ -28,7 +29,6 @@ def tile_dft_w_kernel(tc, x, real_words, real_scales, imag_words, imag_scales, o
     scales = (real_scales, imag_scales)
     with ExitStack() as ctx:
         keep = ctx.enter_context(tc.tile_pool(name="keep", bufs=1))
-        work = ctx.enter_context(tc.tile_pool(name="work", bufs=3))
         psum = ctx.enter_context(tc.psum_pool(name="psum", bufs=1))
 
         x_sb = keep.tile([P, K], BF16, align_bytes=64)
@@ -45,28 +45,34 @@ def tile_dft_w_kernel(tc, x, real_words, real_scales, imag_words, imag_scales, o
         ident = keep.tile([P, P], F32)
         make_identity(nc, ident[:])
 
-        for w in range(2):
+        def load_scales(w):
             for q in range(4):
                 nc.sync.dma_start(
                     out=planes[32 * q : 32 * q + 16, w, :].bitcast(I32),
                     in_=scales[w][:, 4 * q : 4 * q + 4, :].bitcast(I32),
                 )
 
-        rhs = {}
-        order = [(w, g) for g in range(GROUPS) for w in range(2)]
-        for w, g in order[:WHOLE]:
+        whole = {}
+
+        def load_whole(w, g):
             wt = keep.tile([P, N], U32, name="whole%d_%d" % (w, g), align_bytes=64)
             nc.sync.dma_start(out=wt[:].bitcast(I32), in_=words[w][g].rearrange("p n t -> p (n t)").bitcast(I32))
-            for j in range(N_TILES):
-                rhs[(w, g, j)] = wt[:, N_TILE * j : N_TILE * (j + 1)]
-        for j in range(N_TILES):
-            for w, g in order[WHOLE:]:
-                wt = keep.tile([P, N_TILE], U32, name="late%d_%d_%d" % (w, g, j), align_bytes=64)
-                nc.sync.dma_start(
-                    out=wt[:].bitcast(I32),
-                    in_=words[w][g].rearrange("p n t -> p (n t)")[:, 4 * N_TILE * j : 4 * N_TILE * (j + 1)].bitcast(I32),
-                )
-                rhs[(w, g, j)] = wt[:]
+            whole[(w, g)] = wt
+
+        load_scales(REAL)
+        for g in range(GROUPS):
+            load_whole(REAL, g)
+        load_scales(IMAG)
+        for g in range(WHOLE_IMAG):
+            load_whole(IMAG, g)
+        late = []
+        late_view = imag_words.rearrange("g p n t -> p g (n t)")
+        for n0, width in IMAG_RANGES:
+            wt = keep.tile([P, GROUPS - WHOLE_IMAG, width], U32, name="late%d" % n0, align_bytes=64)
+            nc.sync.dma_start(
+                out=wt[:].bitcast(I32), in_=late_view[:, WHOLE_IMAG:GROUPS, 4 * n0 : 4 * (n0 + width)].bitcast(I32)
+            )
+            late.append(wt)
 
         xw = x_sb[:].bitcast(F32)
         grouped = keep.tile([P, K], BF16, align_bytes=64)
@@ -74,7 +80,7 @@ def tile_dft_w_kernel(tc, x, real_words, real_scales, imag_words, imag_scales, o
         x_codes = keep.tile([P, GROUPS * P], U32, align_bytes=64)
         x_plane = keep.tile([P, GROUPS * P], U8, align_bytes=64)
         for h in range(2):
-            xt = psum.tile([P, 4, P], F32, tag="acc1_%d" % (2 + h), name="xt%d" % h)
+            xt = psum.tile([P, 4, P], F32, tag="bank%d" % (4 + h), name="xt%d" % h)
             for gl in range(2):
                 g = 2 * h + gl
                 for u in range(2):
@@ -92,41 +98,49 @@ def tile_dft_w_kernel(tc, x, real_words, real_scales, imag_words, imag_scales, o
                 in_=grouped[:, 1024 * h : 1024 * (h + 1)],
             )
 
-        acc = {}
-        for w in range(2):
-            for j in range(N_TILES):
-                acc[(w, j)] = psum.tile([P, N_TILE], F32, tag="acc%d_%d" % (w, j), name="acc%d_%d" % (w, j))
-
-        def mx_pass(w, g, j):
+        def mx_pass(acc, w, g, rhs, n0, width):
             nc.tensor.matmul_mx(
-                out=acc[(w, j)][:],
+                out=acc[:],
                 lhsT=x_codes[:, P * g : P * (g + 1)].bitcast(FP8X4),
                 lhsT_scale=x_plane[:, P * g : P * (g + 1)],
-                rhs=rhs[(w, g, j)].bitcast(FP8X4),
-                rhs_scale=planes[4 * g : P, w, N_TILE * j : N_TILE * (j + 1)],
+                rhs=rhs.bitcast(FP8X4),
+                rhs_scale=planes[4 * g : P, w, n0 : n0 + width],
                 start=(g == 0),
                 stop=(g == GROUPS - 1),
             )
 
-        for w, g in order[:WHOLE]:
-            for j in range(N_TILES):
-                mx_pass(w, g, j)
+        square_real = keep.tile([P, N], F32)
+        square_imag = keep.tile([P, N], F32)
+        result = keep.tile([P, N], F32)
 
-        for j in range(N_TILES):
-            parts = 2 if j == N_TILES - 1 else 1
-            width = N_TILE // parts
-            sq = [work.tile([P, N_TILE], F32, tag="sq%d" % w, name="sq%d_%d" % (w, j)) for w in range(2)]
-            res = work.tile([P, N_TILE], F32, tag="res")
-            for w, g in order[WHOLE:]:
-                mx_pass(w, g, j)
-                if g == GROUPS - 1:
-                    for c in range(parts):
-                        cols = slice(width * c, width * (c + 1))
-                        nc.scalar.activation(out=sq[w][:, cols], in_=acc[(w, j)][:, cols], func=ACT.Square)
-            for c in range(parts):
-                cols = slice(width * c, width * (c + 1))
-                nc.vector.tensor_tensor(out=sq[1][:, cols], in0=sq[1][:, cols], in1=sq[0][:, cols], op=ALU.add)
-                nc.scalar.activation(out=res[:, cols], in_=sq[1][:, cols], func=ACT.Ln)
-                nc.scalar.dma_start(
-                    out=out[:, N_TILE * j + width * c : N_TILE * j + width * (c + 1)], in_=res[:, cols]
+        acc_real = [psum.tile([P, BANK], F32, tag="bank%d" % j, name="real%d" % j) for j in range(N // BANK)]
+        for g in range(GROUPS):
+            for j in range(N // BANK):
+                mx_pass(acc_real[j], REAL, g, whole[(REAL, g)][:, BANK * j : BANK * (j + 1)], BANK * j, BANK)
+        for j in range(N // BANK):
+            nc.scalar.activation(out=square_real[:, BANK * j : BANK * (j + 1)], in_=acc_real[j][:], func=ACT.Square)
+
+        acc_imag = [
+            psum.tile([P, width], F32, tag="bank%d" % ((4 + r) % 8), name="imag%d" % r)
+            for r, (n0, width) in enumerate(IMAG_RANGES)
+        ]
+        for g in range(WHOLE_IMAG):
+            for r, (n0, width) in enumerate(IMAG_RANGES):
+                mx_pass(acc_imag[r], IMAG, g, whole[(IMAG, g)][:, n0 : n0 + width], n0, width)
+        for r, (n0, width) in enumerate(IMAG_RANGES):
+            for g in range(WHOLE_IMAG, GROUPS):
+                mx_pass(acc_imag[r], IMAG, g, late[r][:, g - WHOLE_IMAG, :], n0, width)
+            half = width // 2
+            for c in range(2):
+                nc.scalar.activation(
+                    out=square_imag[:, n0 + half * c : n0 + half * (c + 1)],
+                    in_=acc_imag[r][:, half * c : half * (c + 1)],
+                    func=ACT.Square,
                 )
+            for c in range(2):
+                cols = slice(n0 + half * c, n0 + half * (c + 1))
+                nc.vector.tensor_tensor(
+                    out=square_imag[:, cols], in0=square_imag[:, cols], in1=square_real[:, cols], op=ALU.add
+                )
+                nc.scalar.activation(out=result[:, cols], in_=square_imag[:, cols], func=ACT.Ln)
+            nc.sync.dma_start(out=out[:, n0 : n0 + width], in_=result[:, n0 : n0 + width])

@@ -18,8 +18,7 @@ N = 2048
 GROUPS = K // 512
 BANK = 512
 REAL, IMAG = 0, 1
-WHOLE_IMAG = 1
-IMAG_RANGES = [(0, 512), (512, 512), (1024, 512), (1536, 256), (1792, 256)]
+N_FIRST = 1536
 FLOPS = 2 * 2 * P * K * N
 
 
@@ -45,34 +44,47 @@ def tile_dft_w_kernel(tc, x, real_words, real_scales, imag_words, imag_scales, o
         ident = keep.tile([P, P], F32)
         make_identity(nc, ident[:])
 
-        def load_scales(w):
+        def load_scales(w, queue):
             for q in range(4):
+                if queue == "gpsimd":
+                    nc.gpsimd.dma_start(
+                        out=planes[32 * q : 32 * q + 16, w, :].bitcast(F32),
+                        in_=scales[w][:, 4 * q : 4 * q + 4, :].bitcast(F32),
+                    )
+                else:
+                    nc.sync.dma_start(
+                        out=planes[32 * q : 32 * q + 16, w, :].bitcast(I32),
+                        in_=scales[w][:, 4 * q : 4 * q + 4, :].bitcast(I32),
+                    )
+
+        rhs = {}
+
+        def load_first(w):
+            for g in range(GROUPS):
+                wt = keep.tile([P, N_FIRST], U32, name="first%d_%d" % (w, g), align_bytes=64)
                 nc.sync.dma_start(
-                    out=planes[32 * q : 32 * q + 16, w, :].bitcast(I32),
-                    in_=scales[w][:, 4 * q : 4 * q + 4, :].bitcast(I32),
+                    out=wt[:].bitcast(I32),
+                    in_=words[w][g].rearrange("p n t -> p (n t)")[:, : 4 * N_FIRST].bitcast(I32),
                 )
+                for j in range(N_FIRST // BANK):
+                    rhs[(w, g, j)] = wt[:, BANK * j : BANK * (j + 1)]
 
-        whole = {}
-
-        def load_whole(w, g):
-            wt = keep.tile([P, N], U32, name="whole%d_%d" % (w, g), align_bytes=64)
-            nc.sync.dma_start(out=wt[:].bitcast(I32), in_=words[w][g].rearrange("p n t -> p (n t)").bitcast(I32))
-            whole[(w, g)] = wt
-
-        load_scales(REAL)
-        for g in range(GROUPS):
-            load_whole(REAL, g)
-        load_scales(IMAG)
-        for g in range(WHOLE_IMAG):
-            load_whole(IMAG, g)
-        late = []
-        late_view = imag_words.rearrange("g p n t -> p g (n t)")
-        for n0, width in IMAG_RANGES:
-            wt = keep.tile([P, GROUPS - WHOLE_IMAG, width], U32, name="late%d" % n0, align_bytes=64)
+        def load_last(w, g0, ng):
+            wt = keep.tile([P, ng, N - N_FIRST], U32, name="last%d_%d" % (w, g0), align_bytes=64)
             nc.sync.dma_start(
-                out=wt[:].bitcast(I32), in_=late_view[:, WHOLE_IMAG:GROUPS, 4 * n0 : 4 * (n0 + width)].bitcast(I32)
+                out=wt[:].bitcast(I32),
+                in_=words[w].rearrange("g p n t -> p g (n t)")[:, g0 : g0 + ng, 4 * N_FIRST :].bitcast(I32),
             )
-            late.append(wt)
+            for g in range(g0, g0 + ng):
+                rhs[(w, g, N_FIRST // BANK)] = wt[:, g - g0, :]
+
+        load_scales(REAL, "sync")
+        load_first(REAL)
+        load_scales(IMAG, "sync")
+        load_first(IMAG)
+        load_last(REAL, 0, GROUPS)
+        load_last(IMAG, 0, GROUPS - 1)
+        load_last(IMAG, GROUPS - 1, 1)
 
         xw = x_sb[:].bitcast(F32)
         grouped = keep.tile([P, K], BF16, align_bytes=64)
@@ -80,7 +92,7 @@ def tile_dft_w_kernel(tc, x, real_words, real_scales, imag_words, imag_scales, o
         x_codes = keep.tile([P, GROUPS * P], U32, align_bytes=64)
         x_plane = keep.tile([P, GROUPS * P], U8, align_bytes=64)
         for h in range(2):
-            xt = psum.tile([P, 4, P], F32, tag="bank%d" % (4 + h), name="xt%d" % h)
+            xt = psum.tile([P, 4, P], F32, tag="acc1_%d" % (2 + h), name="xt%d" % h)
             for gl in range(2):
                 g = 2 * h + gl
                 for u in range(2):
@@ -98,49 +110,54 @@ def tile_dft_w_kernel(tc, x, real_words, real_scales, imag_words, imag_scales, o
                 in_=grouped[:, 1024 * h : 1024 * (h + 1)],
             )
 
-        def mx_pass(acc, w, g, rhs, n0, width):
-            nc.tensor.matmul_mx(
-                out=acc[:],
-                lhsT=x_codes[:, P * g : P * (g + 1)].bitcast(FP8X4),
-                lhsT_scale=x_plane[:, P * g : P * (g + 1)],
-                rhs=rhs.bitcast(FP8X4),
-                rhs_scale=planes[4 * g : P, w, n0 : n0 + width],
-                start=(g == 0),
-                stop=(g == GROUPS - 1),
-            )
-
-        square_real = keep.tile([P, N], F32)
-        square_imag = keep.tile([P, N], F32)
+        acc = {}
+        for w in (REAL, IMAG):
+            for j in range(N // BANK):
+                acc[(w, j)] = psum.tile([P, BANK], F32, tag="acc%d_%d" % (w, j), name="acc%d_%d" % (w, j))
+        square = [keep.tile([P, N], F32, name="square%d" % w) for w in (REAL, IMAG)]
         result = keep.tile([P, N], F32)
 
-        acc_real = [psum.tile([P, BANK], F32, tag="bank%d" % j, name="real%d" % j) for j in range(N // BANK)]
-        for g in range(GROUPS):
-            for j in range(N // BANK):
-                mx_pass(acc_real[j], REAL, g, whole[(REAL, g)][:, BANK * j : BANK * (j + 1)], BANK * j, BANK)
-        for j in range(N // BANK):
-            nc.scalar.activation(out=square_real[:, BANK * j : BANK * (j + 1)], in_=acc_real[j][:], func=ACT.Square)
+        def project(w, banks):
+            for g in range(GROUPS):
+                for j in banks:
+                    nc.tensor.matmul_mx(
+                        out=acc[(w, j)][:],
+                        lhsT=x_codes[:, P * g : P * (g + 1)].bitcast(FP8X4),
+                        lhsT_scale=x_plane[:, P * g : P * (g + 1)],
+                        rhs=rhs[(w, g, j)].bitcast(FP8X4),
+                        rhs_scale=planes[4 * g : P, w, BANK * j : BANK * (j + 1)],
+                        start=(g == 0),
+                        stop=(g == GROUPS - 1),
+                    )
 
-        acc_imag = [
-            psum.tile([P, width], F32, tag="bank%d" % ((4 + r) % 8), name="imag%d" % r)
-            for r, (n0, width) in enumerate(IMAG_RANGES)
-        ]
-        for g in range(WHOLE_IMAG):
-            for r, (n0, width) in enumerate(IMAG_RANGES):
-                mx_pass(acc_imag[r], IMAG, g, whole[(IMAG, g)][:, n0 : n0 + width], n0, width)
-        for r, (n0, width) in enumerate(IMAG_RANGES):
-            for g in range(WHOLE_IMAG, GROUPS):
-                mx_pass(acc_imag[r], IMAG, g, late[r][:, g - WHOLE_IMAG, :], n0, width)
-            half = width // 2
-            for c in range(2):
-                nc.scalar.activation(
-                    out=square_imag[:, n0 + half * c : n0 + half * (c + 1)],
-                    in_=acc_imag[r][:, half * c : half * (c + 1)],
-                    func=ACT.Square,
-                )
-            for c in range(2):
-                cols = slice(n0 + half * c, n0 + half * (c + 1))
-                nc.vector.tensor_tensor(
-                    out=square_imag[:, cols], in0=square_imag[:, cols], in1=square_real[:, cols], op=ALU.add
-                )
-                nc.scalar.activation(out=result[:, cols], in_=square_imag[:, cols], func=ACT.Ln)
-            nc.sync.dma_start(out=out[:, n0 : n0 + width], in_=result[:, n0 : n0 + width])
+        def square_of(w, j, c0, width):
+            nc.scalar.activation(
+                out=square[w][:, BANK * j + c0 : BANK * j + c0 + width], in_=acc[(w, j)][:, c0 : c0 + width], func=ACT.Square
+            )
+
+        def log_of_sum(n0, width):
+            cols = slice(n0, n0 + width)
+            nc.vector.tensor_tensor(out=square[IMAG][:, cols], in0=square[IMAG][:, cols], in1=square[REAL][:, cols], op=ALU.add)
+            nc.scalar.activation(out=result[:, cols], in_=square[IMAG][:, cols], func=ACT.Ln)
+
+        first = range(N_FIRST // BANK)
+        last = N_FIRST // BANK
+        project(REAL, first)
+        for j in first:
+            square_of(REAL, j, 0, BANK)
+        project(IMAG, first)
+        for j in first:
+            square_of(IMAG, j, 0, BANK)
+        for j in first:
+            log_of_sum(BANK * j, BANK)
+        nc.sync.dma_start(out=out[:, :N_FIRST], in_=result[:, :N_FIRST])
+
+        project(REAL, [last])
+        square_of(REAL, last, 0, BANK)
+        project(IMAG, [last])
+        half = BANK // 2
+        for c in range(2):
+            square_of(IMAG, last, half * c, half)
+        for c in range(2):
+            log_of_sum(N_FIRST + half * c, half)
+        nc.sync.dma_start(out=out[:, N_FIRST:], in_=result[:, N_FIRST:])

@@ -78,9 +78,9 @@ def tile_dft_w_kernel(tc, x, real_words, real_scales, imag_words, imag_scales, o
             for g in range(g0, g0 + ng):
                 rhs[(w, g, N_FIRST // BANK)] = wt[:, g - g0, :]
 
-        load_scales(REAL, "sync")
+        load_scales(REAL, "gpsimd")
         load_first(REAL)
-        load_scales(IMAG, "sync")
+        load_scales(IMAG, "gpsimd")
         load_first(IMAG)
         load_last(REAL, 0, GROUPS)
         load_last(IMAG, 0, GROUPS - 1)

@@ -159,5 +159,6 @@ def tile_dft_w_kernel(tc, x, real_words, real_scales, imag_words, imag_scales, o
         for c in range(2):
             square_of(IMAG, last, half * c, half)
         for c in range(2):
+            cols = slice(N_FIRST + half * c, N_FIRST + half * (c + 1))
             log_of_sum(N_FIRST + half * c, half)
-        nc.sync.dma_start(out=out[:, N_FIRST:], in_=result[:, N_FIRST:])
+            nc.sync.dma_start(out=out[:, cols], in_=result[:, cols])

@@ -18,14 +18,17 @@ N = 2048
 GROUPS = K // 512
 BANK = 512
 REAL, IMAG = 0, 1
-N_FIRST = 1536
+PART_ONE = N - BANK
+REAL_RANGES = [(n0, BANK) for n0 in range(0, N, BANK)]
+IMAG_RANGES = [(n0, BANK) for n0 in range(0, PART_ONE, BANK)] + [(PART_ONE, BANK // 2), (PART_ONE + BANK // 2, BANK // 2)]
+PSUM_BANKS = 8
 FLOPS = 2 * 2 * P * K * N
 
 
-def tile_dft_w_kernel(tc, x, real_words, real_scales, imag_words, imag_scales, out):
+def tile_dft_w_kernel(tc, x, dft_real_words, dft_real_scales, dft_imag_words, dft_imag_scales, out):
     nc = tc.nc
-    words = (real_words, imag_words)
-    scales = (real_scales, imag_scales)
+    words = (dft_real_words, dft_imag_words)
+    scales = (dft_real_scales, dft_imag_scales)
     with ExitStack() as ctx:
         keep = ctx.enter_context(tc.tile_pool(name="keep", bufs=1))
         psum = ctx.enter_context(tc.psum_pool(name="psum", bufs=1))
@@ -44,121 +47,105 @@ def tile_dft_w_kernel(tc, x, real_words, real_scales, imag_words, imag_scales, o
         ident = keep.tile([P, P], F32)
         make_identity(nc, ident[:])
 
-        def load_scales(w, queue):
-            for q in range(4):
-                if queue == "gpsimd":
-                    nc.gpsimd.dma_start(
-                        out=planes[32 * q : 32 * q + 16, w, :].bitcast(F32),
-                        in_=scales[w][:, 4 * q : 4 * q + 4, :].bitcast(F32),
-                    )
-                else:
-                    nc.sync.dma_start(
-                        out=planes[32 * q : 32 * q + 16, w, :].bitcast(I32),
-                        in_=scales[w][:, 4 * q : 4 * q + 4, :].bitcast(I32),
-                    )
-
-        rhs = {}
-
-        def load_first(w):
-            for g in range(GROUPS):
-                wt = keep.tile([P, N_FIRST], U32, name="first%d_%d" % (w, g), align_bytes=64)
-                nc.sync.dma_start(
-                    out=wt[:].bitcast(I32),
-                    in_=words[w][g].rearrange("p n t -> p (n t)")[:, : 4 * N_FIRST].bitcast(I32),
+        for w in (REAL, IMAG):
+            for quadrant in range(4):
+                nc.gpsimd.dma_start(
+                    out=planes[32 * quadrant : 32 * quadrant + 16, w, :].bitcast(F32),
+                    in_=scales[w][:, 4 * quadrant : 4 * quadrant + 4, :].bitcast(F32),
                 )
-                for j in range(N_FIRST // BANK):
-                    rhs[(w, g, j)] = wt[:, BANK * j : BANK * (j + 1)]
 
-        def load_last(w, g0, ng):
-            wt = keep.tile([P, ng, N - N_FIRST], U32, name="last%d_%d" % (w, g0), align_bytes=64)
+        held = {(w, g): [] for w in (REAL, IMAG) for g in range(GROUPS)}
+
+        def load_words(w, g0, n_groups, n0, width):
+            piece = keep.tile([P, n_groups, width], U32, name="words%d_%d_%d" % (w, g0, n0), align_bytes=64)
             nc.sync.dma_start(
-                out=wt[:].bitcast(I32),
-                in_=words[w].rearrange("g p n t -> p g (n t)")[:, g0 : g0 + ng, 4 * N_FIRST :].bitcast(I32),
+                out=piece[:].bitcast(I32),
+                in_=words[w].rearrange("g p n t -> p g (n t)")[:, g0 : g0 + n_groups, 4 * n0 : 4 * (n0 + width)].bitcast(I32),
             )
-            for g in range(g0, g0 + ng):
-                rhs[(w, g, N_FIRST // BANK)] = wt[:, g - g0, :]
+            for g in range(g0, g0 + n_groups):
+                held[(w, g)].append((n0, width, piece[:, g - g0, :]))
 
-        load_scales(REAL, "gpsimd")
-        load_first(REAL)
-        load_scales(IMAG, "gpsimd")
-        load_first(IMAG)
-        load_last(REAL, 0, GROUPS)
-        load_last(IMAG, 0, GROUPS - 1)
-        load_last(IMAG, GROUPS - 1, 1)
+        for w in (REAL, IMAG):
+            for g in range(GROUPS):
+                load_words(w, g, 1, 0, PART_ONE)
+        load_words(REAL, 0, GROUPS, PART_ONE, BANK)
+        load_words(IMAG, 0, GROUPS - 1, PART_ONE, BANK)
+        for n0, width in IMAG_RANGES:
+            if n0 >= PART_ONE:
+                load_words(IMAG, GROUPS - 1, 1, n0, width)
 
-        xw = x_sb[:].bitcast(F32)
+        x_words = x_sb[:].bitcast(F32)
         grouped = keep.tile([P, K], BF16, align_bytes=64)
-        grouped_w = grouped[:].bitcast(F32)
+        grouped_words = grouped[:].bitcast(F32)
         x_codes = keep.tile([P, GROUPS * P], U32, align_bytes=64)
         x_plane = keep.tile([P, GROUPS * P], U8, align_bytes=64)
-        for h in range(2):
-            xt = psum.tile([P, 4, P], F32, tag="acc1_%d" % (2 + h), name="xt%d" % h)
-            for gl in range(2):
-                g = 2 * h + gl
+        for pair in range(GROUPS // 2):
+            flipped = psum.tile([P, 4, P], F32, tag="bank%d" % (4 + pair), name="flipped%d" % pair)
+            for i in range(2):
+                g = 2 * pair + i
                 for u in range(2):
-                    nc.tensor.transpose(xt[:, 2 * gl + u, :], xw[:, 256 * g + u : 256 * (g + 1) : 2], ident[:])
-            dst = grouped_w[:, 512 * h : 512 * (h + 1)].rearrange("p (g b u) -> p g b u", g=2, u=2)
-            src = xt[:].rearrange("p (g u) b -> p g b u", u=2)
-            if h == 0:
+                    nc.tensor.transpose(flipped[:, 2 * i + u, :], x_words[:, 256 * g + u : 256 * (g + 1) : 2], ident[:])
+            dst = grouped_words[:, 512 * pair : 512 * (pair + 1)].rearrange("p (g b u) -> p g b u", g=2, u=2)
+            src = flipped[:].rearrange("p (g u) b -> p g b u", u=2)
+            if pair == 0:
                 nc.vector.tensor_copy(out=dst, in_=src)
             else:
                 nc.scalar.copy(out=dst, in_=src)
-        for h in range(2):
+        for pair in range(GROUPS // 2):
             nc.vector.quantize_mx(
-                out=x_codes[:, 256 * h : 256 * (h + 1)].bitcast(FP8X4),
-                scales=x_plane[:, 256 * h : 256 * (h + 1)],
-                in_=grouped[:, 1024 * h : 1024 * (h + 1)],
+                out=x_codes[:, 2 * P * pair : 2 * P * (pair + 1)].bitcast(FP8X4),
+                scales=x_plane[:, 2 * P * pair : 2 * P * (pair + 1)],
+                in_=grouped[:, 8 * P * pair : 8 * P * (pair + 1)],
             )
 
         acc = {}
-        for w in (REAL, IMAG):
-            for j in range(N // BANK):
-                acc[(w, j)] = psum.tile([P, BANK], F32, tag="acc%d_%d" % (w, j), name="acc%d_%d" % (w, j))
+        for r, (n0, width) in enumerate(REAL_RANGES):
+            acc[(REAL, n0)] = psum.tile([P, width], F32, tag="bank%d" % r, name="real%d" % n0)
+        for r, (n0, width) in enumerate(IMAG_RANGES):
+            acc[(IMAG, n0)] = psum.tile([P, width], F32, tag="bank%d" % ((4 + r) % PSUM_BANKS), name="imag%d" % n0)
         square = [keep.tile([P, N], F32, name="square%d" % w) for w in (REAL, IMAG)]
         result = keep.tile([P, N], F32)
 
-        def project(w, banks):
-            for g in range(GROUPS):
-                for j in banks:
-                    nc.tensor.matmul_mx(
-                        out=acc[(w, j)][:],
-                        lhsT=x_codes[:, P * g : P * (g + 1)].bitcast(FP8X4),
-                        lhsT_scale=x_plane[:, P * g : P * (g + 1)],
-                        rhs=rhs[(w, g, j)].bitcast(FP8X4),
-                        rhs_scale=planes[4 * g : P, w, BANK * j : BANK * (j + 1)],
-                        start=(g == 0),
-                        stop=(g == GROUPS - 1),
-                    )
-
-        def square_of(w, j, c0, width):
-            nc.scalar.activation(
-                out=square[w][:, BANK * j + c0 : BANK * j + c0 + width], in_=acc[(w, j)][:, c0 : c0 + width], func=ACT.Square
+        def mx_pass(w, g, n0, width):
+            for start, size, piece in held[(w, g)]:
+                if start <= n0 and n0 + width <= start + size:
+                    moving = piece[:, n0 - start : n0 - start + width]
+            nc.tensor.matmul_mx(
+                out=acc[(w, n0)][:],
+                lhsT=x_codes[:, P * g : P * (g + 1)].bitcast(FP8X4),
+                lhsT_scale=x_plane[:, P * g : P * (g + 1)],
+                rhs=moving.bitcast(FP8X4),
+                rhs_scale=planes[4 * g : P, w, n0 : n0 + width],
+                start=(g == 0),
+                stop=(g == GROUPS - 1),
             )
+
+        def project(w, ranges):
+            for g in range(GROUPS):
+                for n0, width in ranges:
+                    mx_pass(w, g, n0, width)
+
+        def square_of(w, ranges):
+            for n0, width in ranges:
+                nc.scalar.activation(out=square[w][:, n0 : n0 + width], in_=acc[(w, n0)][:], func=ACT.Square)
 
         def log_of_sum(n0, width):
             cols = slice(n0, n0 + width)
             nc.vector.tensor_tensor(out=square[IMAG][:, cols], in0=square[IMAG][:, cols], in1=square[REAL][:, cols], op=ALU.add)
             nc.scalar.activation(out=result[:, cols], in_=square[IMAG][:, cols], func=ACT.Ln)
 
-        first = range(N_FIRST // BANK)
-        last = N_FIRST // BANK
-        project(REAL, first)
-        for j in first:
-            square_of(REAL, j, 0, BANK)
-        project(IMAG, first)
-        for j in first:
-            square_of(IMAG, j, 0, BANK)
-        for j in first:
-            log_of_sum(BANK * j, BANK)
-        nc.sync.dma_start(out=out[:, :N_FIRST], in_=result[:, :N_FIRST])
-
-        project(REAL, [last])
-        square_of(REAL, last, 0, BANK)
-        project(IMAG, [last])
-        half = BANK // 2
-        for c in range(2):
-            square_of(IMAG, last, half * c, half)
-        for c in range(2):
-            cols = slice(N_FIRST + half * c, N_FIRST + half * (c + 1))
-            log_of_sum(N_FIRST + half * c, half)
-            nc.sync.dma_start(out=out[:, cols], in_=result[:, cols])
+        for in_part in (lambda n0: n0 < PART_ONE, lambda n0: n0 >= PART_ONE):
+            real_ranges = [rng for rng in REAL_RANGES if in_part(rng[0])]
+            imag_ranges = [rng for rng in IMAG_RANGES if in_part(rng[0])]
+            project(REAL, real_ranges)
+            square_of(REAL, real_ranges)
+            project(IMAG, imag_ranges)
+            square_of(IMAG, imag_ranges)
+            if in_part(0):
+                for n0, width in imag_ranges:
+                    log_of_sum(n0, width)
+                nc.sync.dma_start(out=out[:, :PART_ONE], in_=result[:, :PART_ONE])
+            else:
+                for n0, width in imag_ranges:
+                    log_of_sum(n0, width)
+                    nc.sync.dma_start(out=out[:, n0 : n0 + width], in_=result[:, n0 : n0 + width])

@@ -20,7 +20,7 @@ BANK = 512
 REAL, IMAG = 0, 1
 PART_ONE = N - BANK
 REAL_RANGES = [(n0, BANK) for n0 in range(0, N, BANK)]
-IMAG_RANGES = [(n0, BANK) for n0 in range(0, PART_ONE, BANK)] + [(PART_ONE, BANK // 2), (PART_ONE + BANK // 2, BANK // 2)]
+IMAG_RANGES = [(n0, BANK) for n0 in range(0, PART_ONE, BANK)] + [(PART_ONE, 256), (PART_ONE + 256, 128), (PART_ONE + 384, 128)]
 PSUM_BANKS = 8
 FLOPS = 2 * 2 * P * K * N
 
@@ -69,10 +69,10 @@ def tile_dft_w_kernel(tc, x, dft_real_words, dft_real_scales, dft_imag_words, df
             for g in range(GROUPS):
                 load_words(w, g, 1, 0, PART_ONE)
         load_words(REAL, 0, GROUPS, PART_ONE, BANK)
-        load_words(IMAG, 0, GROUPS - 1, PART_ONE, BANK)
-        for n0, width in IMAG_RANGES:
-            if n0 >= PART_ONE:
-                load_words(IMAG, GROUPS - 1, 1, n0, width)
+        load_words(IMAG, 0, GROUPS, PART_ONE, 256)
+        load_words(IMAG, 0, GROUPS - 1, PART_ONE + 256, 256)
+        load_words(IMAG, GROUPS - 1, 1, PART_ONE + 256, 128)
+        load_words(IMAG, GROUPS - 1, 1, PART_ONE + 384, 128)
 
         x_words = x_sb[:].bitcast(F32)
         grouped = keep.tile([P, K], BF16, align_bytes=64)
@@ -139,7 +139,11 @@ def tile_dft_w_kernel(tc, x, dft_real_words, dft_real_scales, dft_imag_words, df
             imag_ranges = [rng for rng in IMAG_RANGES if in_part(rng[0])]
             project(REAL, real_ranges)
             square_of(REAL, real_ranges)
-            project(IMAG, imag_ranges)
+            if in_part(0):
+                project(IMAG, imag_ranges)
+            else:
+                project(IMAG, imag_ranges[:1])
+                project(IMAG, imag_ranges[1:])
             square_of(IMAG, imag_ranges)
             if in_part(0):
                 for n0, width in imag_ranges:

@@ -148,7 +148,7 @@ def tile_dft_w_kernel(tc, x, dft_real_words, dft_real_scales, dft_imag_words, df
             if in_part(0):
                 for n0, width in imag_ranges:
                     log_of_sum(n0, width)
-                nc.sync.dma_start(out=out[:, :PART_ONE], in_=result[:, :PART_ONE])
+                    nc.sync.dma_start(out=out[:, n0 : n0 + width], in_=result[:, n0 : n0 + width])
             else:
                 for n0, width in imag_ranges:
                     log_of_sum(n0, width)

@@ -33,10 +33,10 @@ def tile_dft_w_kernel(tc, x, dft_real_words, dft_real_scales, dft_imag_words, df
         keep = ctx.enter_context(tc.tile_pool(name="keep", bufs=1))
         psum = ctx.enter_context(tc.psum_pool(name="psum", bufs=1))
 
-        x_sb = keep.tile([P, K], BF16, align_bytes=64)
+        x_sb = keep.tile([P, K], BF16, align_bytes=256)
         nc.sync.dma_start(out=x_sb[:], in_=x)
 
-        planes = keep.tile([P, 2, N], U8, align_bytes=64)
+        planes = keep.tile([P, 2, N], U8, align_bytes=256)
         nc.vector.memset(planes[:].rearrange("p w n -> p (w n)").bitcast(I32), 0)
 
         one = keep.tile([P, 1], F32)
@@ -57,7 +57,7 @@ def tile_dft_w_kernel(tc, x, dft_real_words, dft_real_scales, dft_imag_words, df
         held = {(w, g): [] for w in (REAL, IMAG) for g in range(GROUPS)}
 
         def load_words(w, g0, n_groups, n0, width):
-            piece = keep.tile([P, n_groups, width], U32, name="words%d_%d_%d" % (w, g0, n0), align_bytes=64)
+            piece = keep.tile([P, n_groups, width], U32, name="words%d_%d_%d" % (w, g0, n0), align_bytes=256)
             nc.sync.dma_start(
                 out=piece[:].bitcast(I32),
                 in_=words[w].rearrange("g p n t -> p g (n t)")[:, g0 : g0 + n_groups, 4 * n0 : 4 * (n0 + width)].bitcast(I32),
@@ -104,7 +104,7 @@ def tile_dft_w_kernel(tc, x, dft_real_words, dft_real_scales, dft_imag_words, df
         for r, (n0, width) in enumerate(IMAG_RANGES):
             acc[(IMAG, n0)] = psum.tile([P, width], F32, tag="bank%d" % ((4 + r) % PSUM_BANKS), name="imag%d" % n0)
         square = [keep.tile([P, N], F32, name="square%d" % w) for w in (REAL, IMAG)]
-        result = keep.tile([P, N], F32)
+        result = keep.tile([P, N], F32, align_bytes=256)
 
         def mx_pass(w, g, n0, width):
             for start, size, piece in held[(w, g)]:

from contextlib import ExitStack

import concourse.mybir as mybir
from concourse.masks import make_identity

F32 = mybir.dt.float32
BF16 = mybir.dt.bfloat16
I32 = mybir.dt.int32
U32 = mybir.dt.uint32
U8 = mybir.dt.uint8
FP8X4 = mybir.dt.float8_e4m3fn_x4
ACT = mybir.ActivationFunctionType
ALU = mybir.AluOpType

P = 128
K = 2048
N = 2048
GROUPS = K // 512
BANK = 512
REAL, IMAG = 0, 1
PART_ONE = N - BANK
REAL_RANGES = [(n0, BANK) for n0 in range(0, N, BANK)]
IMAG_RANGES = [(n0, BANK) for n0 in range(0, PART_ONE, BANK)] + [(PART_ONE, 256), (PART_ONE + 256, 128), (PART_ONE + 384, 128)]
PSUM_BANKS = 8
FLOPS = 2 * 2 * P * K * N


def tile_dft_w_kernel(tc, x, dft_real_words, dft_real_scales, dft_imag_words, dft_imag_scales, out):
    nc = tc.nc
    words = (dft_real_words, dft_imag_words)
    scales = (dft_real_scales, dft_imag_scales)
    with ExitStack() as ctx:
        keep = ctx.enter_context(tc.tile_pool(name="keep", bufs=1))
        psum = ctx.enter_context(tc.psum_pool(name="psum", bufs=1))

        x_sb = keep.tile([P, K], BF16, align_bytes=256)
        nc.sync.dma_start(out=x_sb[:], in_=x)

        planes = keep.tile([P, 2, N], U8, align_bytes=256)
        nc.vector.memset(planes[:].rearrange("p w n -> p (w n)").bitcast(I32), 0)

        one = keep.tile([P, 1], F32)
        nc.vector.memset(one[:], 1.0)
        warm = keep.tile([P, 1], F32)
        nc.scalar.activation(out=warm[:], in_=one[:], func=ACT.Ln)

        ident = keep.tile([P, P], F32)
        make_identity(nc, ident[:])

        for w in (REAL, IMAG):
            for quadrant in range(4):
                nc.gpsimd.dma_start(
                    out=planes[32 * quadrant : 32 * quadrant + 16, w, :].bitcast(F32),
                    in_=scales[w][:, 4 * quadrant : 4 * quadrant + 4, :].bitcast(F32),
                )

        held = {(w, g): [] for w in (REAL, IMAG) for g in range(GROUPS)}

        def load_words(w, g0, n_groups, n0, width):
            piece = keep.tile([P, n_groups, width], U32, name="words%d_%d_%d" % (w, g0, n0), align_bytes=256)
            nc.sync.dma_start(
                out=piece[:].bitcast(I32),
                in_=words[w].rearrange("g p n t -> p g (n t)")[:, g0 : g0 + n_groups, 4 * n0 : 4 * (n0 + width)].bitcast(I32),
            )
            for g in range(g0, g0 + n_groups):
                held[(w, g)].append((n0, width, piece[:, g - g0, :]))

        for w in (REAL, IMAG):
            for g in range(GROUPS):
                load_words(w, g, 1, 0, PART_ONE)
        load_words(REAL, 0, GROUPS, PART_ONE, BANK)
        load_words(IMAG, 0, GROUPS, PART_ONE, 256)
        load_words(IMAG, 0, GROUPS - 1, PART_ONE + 256, 256)
        load_words(IMAG, GROUPS - 1, 1, PART_ONE + 256, 128)
        load_words(IMAG, GROUPS - 1, 1, PART_ONE + 384, 128)

        x_words = x_sb[:].bitcast(F32)
        grouped = keep.tile([P, K], BF16, align_bytes=64)
        grouped_words = grouped[:].bitcast(F32)
        x_codes = keep.tile([P, GROUPS * P], U32, align_bytes=64)
        x_plane = keep.tile([P, GROUPS * P], U8, align_bytes=64)
        for pair in range(GROUPS // 2):
            flipped = psum.tile([P, 4, P], F32, tag="bank%d" % (4 + pair), name="flipped%d" % pair)
            for i in range(2):
                g = 2 * pair + i
                for u in range(2):
                    nc.tensor.transpose(flipped[:, 2 * i + u, :], x_words[:, 256 * g + u : 256 * (g + 1) : 2], ident[:])
            dst = grouped_words[:, 512 * pair : 512 * (pair + 1)].rearrange("p (g b u) -> p g b u", g=2, u=2)
            src = flipped[:].rearrange("p (g u) b -> p g b u", u=2)
            if pair == 0:
                nc.vector.tensor_copy(out=dst, in_=src)
            else:
                nc.scalar.copy(out=dst, in_=src)
        for pair in range(GROUPS // 2):
            nc.vector.quantize_mx(
                out=x_codes[:, 2 * P * pair : 2 * P * (pair + 1)].bitcast(FP8X4),
                scales=x_plane[:, 2 * P * pair : 2 * P * (pair + 1)],
                in_=grouped[:, 8 * P * pair : 8 * P * (pair + 1)],
            )

        acc = {}
        for r, (n0, width) in enumerate(REAL_RANGES):
            acc[(REAL, n0)] = psum.tile([P, width], F32, tag="bank%d" % r, name="real%d" % n0)
        for r, (n0, width) in enumerate(IMAG_RANGES):
            acc[(IMAG, n0)] = psum.tile([P, width], F32, tag="bank%d" % ((4 + r) % PSUM_BANKS), name="imag%d" % n0)
        square = [keep.tile([P, N], F32, name="square%d" % w) for w in (REAL, IMAG)]
        result = keep.tile([P, N], F32, align_bytes=256)

        def mx_pass(w, g, n0, width):
            for start, size, piece in held[(w, g)]:
                if start <= n0 and n0 + width <= start + size:
                    moving = piece[:, n0 - start : n0 - start + width]
            nc.tensor.matmul_mx(
                out=acc[(w, n0)][:],
                lhsT=x_codes[:, P * g : P * (g + 1)].bitcast(FP8X4),
                lhsT_scale=x_plane[:, P * g : P * (g + 1)],
                rhs=moving.bitcast(FP8X4),
                rhs_scale=planes[4 * g : P, w, n0 : n0 + width],
                start=(g == 0),
                stop=(g == GROUPS - 1),
            )

        def project(w, ranges):
            for g in range(GROUPS):
                for n0, width in ranges:
                    mx_pass(w, g, n0, width)

        def square_of(w, ranges):
            for n0, width in ranges:
                nc.scalar.activation(out=square[w][:, n0 : n0 + width], in_=acc[(w, n0)][:], func=ACT.Square)

        def log_of_sum(n0, width):
            cols = slice(n0, n0 + width)
            nc.vector.tensor_tensor(out=square[IMAG][:, cols], in0=square[IMAG][:, cols], in1=square[REAL][:, cols], op=ALU.add)
            nc.scalar.activation(out=result[:, cols], in_=square[IMAG][:, cols], func=ACT.Ln)

        for in_part in (lambda n0: n0 < PART_ONE, lambda n0: n0 >= PART_ONE):
            real_ranges = [rng for rng in REAL_RANGES if in_part(rng[0])]
            imag_ranges = [rng for rng in IMAG_RANGES if in_part(rng[0])]
            project(REAL, real_ranges)
            square_of(REAL, real_ranges)
            if in_part(0):
                project(IMAG, imag_ranges)
            else:
                project(IMAG, imag_ranges[:1])
                project(IMAG, imag_ranges[1:])
            square_of(IMAG, imag_ranges)
            if in_part(0):
                for n0, width in imag_ranges:
                    log_of_sum(n0, width)
                    nc.sync.dma_start(out=out[:, n0 : n0 + width], in_=result[:, n0 : n0 + width])
            else:
                for n0, width in imag_ranges:
                    log_of_sum(n0, width)
                    nc.sync.dma_start(out=out[:, n0 : n0 + width], in_=result[:, n0 : n0 + width])
